import numpy as np
import ml_dtypes


def mxq(x, axis, fmt="e4m3"):
    dtype, down = {"e4m3": (ml_dtypes.float8_e4m3fn, 7), "e5m2": (ml_dtypes.float8_e5m2, 14)}[fmt]
    v = np.moveaxis(np.asarray(x, np.float32).astype(ml_dtypes.bfloat16).astype(np.float64), axis, -1)
    blocks = v.reshape(v.shape[:-1] + (-1, 32))
    amax = np.abs(blocks).max(-1, keepdims=True)
    byte = np.maximum(np.where(amax > 0, np.frexp(amax)[1] - 1 + 127, 0) - down, 1)
    scale = np.exp2(byte - 127.0)
    codes = (blocks / scale).astype(np.float32).astype(dtype).astype(np.float64)
    return np.moveaxis((codes * scale).reshape(v.shape), -1, axis)


WIDE = False


def mx_kscale(k):
    if not WIDE:
        return np.ones(k)
    levels = np.array([10, -10, 5, -5, 0])
    if k % 512:
        return np.exp2(np.random.permutation(np.resize(levels, k // 32))).repeat(32)
    a = np.empty((k // 512, 16))
    for p in range(k // 512):
        a[p, :8] = np.random.permutation(np.resize(levels, 8))
        for g in range(8):
            far = levels[np.abs(levels - a[p, g]) >= 10]
            a[p, g + 8] = far[np.random.randint(len(far))]
    return np.exp2(a.ravel()).repeat(32)


BF16 = ml_dtypes.bfloat16


def bf(x):
    return np.asarray(x, np.float32).astype(BF16)


def f64(x):
    return np.asarray(x).astype(np.float64)


B, IN, MEM, CTX, H, G = 4096, 512, 512, 1024, 4, 3


def sigmoid(v):
    return 1.0 / (1.0 + np.exp(-v))


def setup_inputs():
    s = mx_kscale(IN)
    w = np.random.standard_normal((MEM, MEM + IN)) / np.sqrt(MEM + IN)
    w[:, MEM:] = w[:, MEM:] / s
    return {"input_tensor": bf(np.random.standard_normal((B, IN)) * s),
            "previous_memory": bf(np.random.standard_normal((B, MEM))),
            "fg_w": bf(w),
            "fg_b": bf(np.random.standard_normal(MEM) * 0.3)}


def reference(input_tensor, previous_memory, fg_w, fg_b):
    m = f64(previous_memory)
    forget_in = np.concatenate([m, f64(input_tensor)], axis=-1)
    fgate = sigmoid((mxq(forget_in, 1, "e4m3") @ mxq(f64(fg_w), 1, "e4m3").T) + f64(fg_b))
    return m * fgate

@@ -1,0 +1,185 @@
+from contextlib import ExitStack
+
+import concourse.mybir as mybir
+from concourse.masks import make_identity
+
+F32 = mybir.dt.float32
+BF16 = mybir.dt.bfloat16
+U32 = mybir.dt.uint32
+U8 = mybir.dt.uint8
+FP8X4 = mybir.dt.float8_e4m3fn_x4
+ADD = mybir.AluOpType.add
+MULT = mybir.AluOpType.mult
+SIGMOID = mybir.ActivationFunctionType.Sigmoid
+
+P = 128
+BATCH = 4096
+FEAT = 512
+PASSES = 2
+PACK = 4
+HALVES = 2
+BLOCKS = PASSES * HALVES
+PASS_WORDS = FEAT // 2
+ROWS_PER_PARTITION = BATCH // P
+GROUP = 2
+GROUPS = ROWS_PER_PARTITION // GROUP
+N_TILES = FEAT // P
+
+FLOPS = 2 * BATCH * (PASSES * FEAT) * FEAT
+
+
+def tile_dynamicmemorycell_pa_t_kernel(tc, input_tensor, previous_memory, fg_w, fg_b, out):
+    nc = tc.nc
+
+    m_rows = previous_memory.rearrange("(p r) k -> p r k", r=ROWS_PER_PARTITION)
+    x_rows = input_tensor.rearrange("(p r) k -> p r k", r=ROWS_PER_PARTITION)
+    out_rows = out.rearrange("(p r) n -> p r n", r=ROWS_PER_PARTITION)
+
+    with ExitStack() as ctx:
+        consts = ctx.enter_context(tc.tile_pool(name="consts", bufs=1))
+        inputs = ctx.enter_context(tc.tile_pool(name="inputs", bufs=GROUPS))
+        stage = ctx.enter_context(tc.tile_pool(name="stage", bufs=3))
+        results = ctx.enter_context(tc.tile_pool(name="results", bufs=GROUPS // 2))
+        psum_t = ctx.enter_context(tc.psum_pool(name="psum_t", bufs=2 * GROUP))
+        psum_acc = ctx.enter_context(tc.psum_pool(name="psum_acc", bufs=2 * GROUP))
+        ctx.enter_context(tc.manual_schedule())
+
+        w_sb = consts.tile([P, N_TILES, PASSES * FEAT], BF16)
+        for j in range(N_TILES):
+            nc.sync.dma_start(out=w_sb[:, j, :], in_=fg_w[j * P : (j + 1) * P, :])
+        bias_row = consts.tile([P, FEAT], BF16)
+        nc.vector.memset(bias_row[:], 0.0)
+        nc.sync.dma_start(out=bias_row[0:1, :], in_=fg_b.rearrange("(o n) -> o n", o=1))
+        m_groups = []
+        x_groups = []
+        for i in range(GROUPS):
+            rows = slice(i * GROUP, (i + 1) * GROUP)
+            m_sb = inputs.tile([P, GROUP, FEAT], BF16)
+            nc.sync.dma_start(out=m_sb[:], in_=m_rows[:, rows, :])
+            x_sb = inputs.tile([P, GROUP, FEAT], BF16)
+            nc.sync.dma_start(out=x_sb[:], in_=x_rows[:, rows, :])
+            m_groups.append(m_sb)
+            x_groups.append(x_sb)
+
+        ident = consts.tile([P, P], F32)
+        make_identity(nc, ident[:])
+        ones = consts.tile([P, P], BF16)
+        nc.vector.memset(ones[:], 1.0)
+        warm = consts.tile([P, 1], F32)
+        nc.vector.memset(warm[:], 0.0)
+        nc.scalar.activation(out=warm[:], in_=warm[:], func=SIGMOID)
+
+        w_words = w_sb[:].bitcast(F32)
+        w_grouped = consts.tile([P, PASSES, FEAT, PACK], BF16, align_bytes=64)
+        w_grouped_words = w_grouped[:].bitcast(F32)
+        for j in range(N_TILES):
+            wt = psum_t.tile([P, BLOCKS, P], F32, tag="xt")
+            for g in range(PASSES):
+                for u in range(HALVES):
+                    words = w_words[:, j, g * PASS_WORDS + u : (g + 1) * PASS_WORDS : HALVES]
+                    nc.tensor.transpose(wt[:, g * HALVES + u, :], words, ident[:])
+            nc.vector.tensor_copy(
+                out=w_grouped_words[:, :, j * P : (j + 1) * P, :],
+                in_=wt[:].rearrange("p (g u) n -> p g n u", u=HALVES),
+            )
+        w_codes = consts.tile([P, PASSES, FEAT], U32, align_bytes=64)
+        w_scales = consts.tile([P, PASSES, FEAT], U8, align_bytes=64)
+        for g in range(PASSES):
+            nc.vector.quantize_mx(
+                out=w_codes[:, g, :].bitcast(FP8X4),
+                scales=w_scales[:, g, :],
+                in_=w_grouped[:, g, :, :].rearrange("p n t -> p (n t)"),
+            )
+
+        bias_sum = psum_acc.tile([P, FEAT], F32, tag="acc")
+        nc.tensor.matmul(out=bias_sum[:], lhsT=ones[:], rhs=bias_row[:], start=True, stop=True)
+        bias = consts.tile([P, FEAT], F32)
+        nc.vector.tensor_copy(out=bias[:], in_=bias_sum[:])
+
+        banks = {}
+        grouped_of = {}
+        codes_of = {}
+        scales_of = {}
+        acc_of = {}
+        z_of = {}
+
+        def transposes(i):
+            for r in range(GROUP):
+                xt = psum_t.tile([P, BLOCKS, P], F32, tag="xt")
+                for g, src in enumerate((m_groups[i], x_groups[i])):
+                    words = src[:].bitcast(F32)
+                    for u in range(HALVES):
+                        nc.tensor.transpose(xt[:, g * HALVES + u, :], words[:, r, u:PASS_WORDS:HALVES], ident[:])
+                banks[(i, r)] = xt
+
+        def regroup(i):
+            grouped = stage.tile([P, GROUP, PASSES, P, PACK], BF16, align_bytes=64)
+            grouped_words = grouped[:].bitcast(F32)
+            for r in range(GROUP):
+                nc.scalar.copy(
+                    out=grouped_words[:, r, :, :, :],
+                    in_=banks[(i, r)][:].rearrange("p (g u) b -> p g b u", u=HALVES),
+                )
+            grouped_of[i] = grouped
+
+        def quantise(i):
+            codes = stage.tile([P, GROUP, PASSES, P], U32, align_bytes=64)
+            scales = stage.tile([P, GROUP, PASSES, P], U8, align_bytes=64)
+            nc.vector.quantize_mx(
+                out=codes[:].rearrange("p r g b -> p (r g b)").bitcast(FP8X4),
+                scales=scales[:].rearrange("p r g b -> p (r g b)"),
+                in_=grouped_of[i][:].rearrange("p r g b t -> p (r g b t)"),
+            )
+            codes_of[i] = codes
+            scales_of[i] = scales
+
+        def matmuls(i):
+            for r in range(GROUP):
+                acc = psum_acc.tile([P, FEAT], F32, tag="acc")
+                for g in range(PASSES):
+                    nc.tensor.matmul_mx(
+                        out=acc[:],
+                        lhsT=codes_of[i][:, r, g, :].bitcast(FP8X4),
+                        lhsT_scale=scales_of[i][:, r, g, :],
+                        rhs=w_codes[:, g, :].bitcast(FP8X4),
+                        rhs_scale=w_scales[:, g, :],
+                        start=(g == 0),
+                        stop=(g == PASSES - 1),
+                    )
+                acc_of[(i, r)] = acc
+
+        def add_bias(i):
+            z = results.tile([P, GROUP, FEAT], F32)
+            for r in range(GROUP):
+                nc.vector.tensor_tensor(out=z[:, r, :], in0=acc_of[(i, r)][:], in1=bias[:], op=ADD)
+            z_of[i] = z
+
+        def gate(i):
+            for r in range(GROUP):
+                nc.scalar.activation(out=z_of[i][:, r, :], in_=z_of[i][:, r, :], func=SIGMOID)
+
+        def multiply_and_store(i):
+            z = z_of[i]
+            engines = (nc.vector if i == GROUPS - 1 else nc.gpsimd, nc.vector)
+            for r in range(GROUP):
+                engines[r].tensor_tensor(out=z[:, r, :], in0=z[:, r, :], in1=m_groups[i][:, r, :], op=MULT)
+                nc.sync.dma_start(out=out_rows[:, i * GROUP + r, :], in_=z[:, r, :])
+
+        transposes(0)
+        regroup(0)
+        quantise(0)
+        for i in range(GROUPS + 1):
+            if i + 1 < GROUPS:
+                transposes(i + 1)
+            if i < GROUPS:
+                matmuls(i)
+            if i + 1 < GROUPS:
+                regroup(i + 1)
+            if i >= 1:
+                gate(i - 1)
+            if i + 1 < GROUPS:
+                quantise(i + 1)
+            if i < GROUPS:
+                add_bias(i)
+            if i >= 1:
+                multiply_and_store(i - 1)

@@ -24,6 +24,8 @@ ROWS_PER_PARTITION = BATCH // P
 GROUP = 2
 GROUPS = ROWS_PER_PARTITION // GROUP
 N_TILES = FEAT // P
+WHOLE = (slice(0, FEAT),)
+HALVED = (slice(0, FEAT // 2), slice(FEAT // 2, FEAT))
 
 FLOPS = 2 * BATCH * (PASSES * FEAT) * FEAT
 
@@ -49,7 +51,6 @@ def tile_dynamicmemorycell_pa_t_kernel(tc, input_tensor, previous_memory, fg_w, 
             nc.sync.dma_start(out=w_sb[:, j, :], in_=fg_w[j * P : (j + 1) * P, :])
         bias_row = consts.tile([P, FEAT], BF16)
         nc.vector.memset(bias_row[:], 0.0)
-        nc.sync.dma_start(out=bias_row[0:1, :], in_=fg_b.rearrange("(o n) -> o n", o=1))
         m_groups = []
         x_groups = []
         for i in range(GROUPS):
@@ -60,6 +61,8 @@ def tile_dynamicmemorycell_pa_t_kernel(tc, input_tensor, previous_memory, fg_w, 
             nc.sync.dma_start(out=x_sb[:], in_=x_rows[:, rows, :])
             m_groups.append(m_sb)
             x_groups.append(x_sb)
+            if i == 0:
+                nc.sync.dma_start(out=bias_row[0:1, :], in_=fg_b.rearrange("(o n) -> o n", o=1))
 
         ident = consts.tile([P, P], F32)
         make_identity(nc, ident[:])
@@ -70,7 +73,7 @@ def tile_dynamicmemorycell_pa_t_kernel(tc, input_tensor, previous_memory, fg_w, 
         nc.scalar.activation(out=warm[:], in_=warm[:], func=SIGMOID)
 
         w_words = w_sb[:].bitcast(F32)
-        w_grouped = consts.tile([P, PASSES, FEAT, PACK], BF16, align_bytes=64)
+        w_grouped = consts.tile([P, N_TILES, PASSES, P, PACK], BF16, align_bytes=64)
         w_grouped_words = w_grouped[:].bitcast(F32)
         for j in range(N_TILES):
             wt = psum_t.tile([P, BLOCKS, P], F32, tag="xt")
@@ -78,23 +81,21 @@ def tile_dynamicmemorycell_pa_t_kernel(tc, input_tensor, previous_memory, fg_w, 
                 for u in range(HALVES):
                     words = w_words[:, j, g * PASS_WORDS + u : (g + 1) * PASS_WORDS : HALVES]
                     nc.tensor.transpose(wt[:, g * HALVES + u, :], words, ident[:])
-            nc.vector.tensor_copy(
-                out=w_grouped_words[:, :, j * P : (j + 1) * P, :],
+            nc.scalar.copy(
+                out=w_grouped_words[:, j, :, :, :],
                 in_=wt[:].rearrange("p (g u) n -> p g n u", u=HALVES),
             )
         w_codes = consts.tile([P, PASSES, FEAT], U32, align_bytes=64)
         w_scales = consts.tile([P, PASSES, FEAT], U8, align_bytes=64)
-        for g in range(PASSES):
-            nc.vector.quantize_mx(
-                out=w_codes[:, g, :].bitcast(FP8X4),
-                scales=w_scales[:, g, :],
-                in_=w_grouped[:, g, :, :].rearrange("p n t -> p (n t)"),
-            )
 
-        bias_sum = psum_acc.tile([P, FEAT], F32, tag="acc")
-        nc.tensor.matmul(out=bias_sum[:], lhsT=ones[:], rhs=bias_row[:], start=True, stop=True)
-        bias = consts.tile([P, FEAT], F32)
-        nc.vector.tensor_copy(out=bias[:], in_=bias_sum[:])
+        def quantise_w(j):
+            cols = slice(j * P, (j + 1) * P)
+            for g in range(PASSES):
+                nc.vector.quantize_mx(
+                    out=w_codes[:, g, cols].bitcast(FP8X4),
+                    scales=w_scales[:, g, cols],
+                    in_=w_grouped[:, j, g, :, :].rearrange("p n t -> p (n t)"),
+                )
 
         banks = {}
         grouped_of = {}
@@ -112,73 +113,97 @@ def tile_dynamicmemorycell_pa_t_kernel(tc, input_tensor, previous_memory, fg_w, 
                         nc.tensor.transpose(xt[:, g * HALVES + u, :], words[:, r, u:PASS_WORDS:HALVES], ident[:])
                 banks[(i, r)] = xt
 
-        def regroup(i):
+        def stage_tiles(i):
             grouped = stage.tile([P, GROUP, PASSES, P, PACK], BF16, align_bytes=64)
-            grouped_words = grouped[:].bitcast(F32)
-            for r in range(GROUP):
-                nc.scalar.copy(
-                    out=grouped_words[:, r, :, :, :],
-                    in_=banks[(i, r)][:].rearrange("p (g u) b -> p g b u", u=HALVES),
-                )
-            grouped_of[i] = grouped
-
-        def quantise(i):
             codes = stage.tile([P, GROUP, PASSES, P], U32, align_bytes=64)
             scales = stage.tile([P, GROUP, PASSES, P], U8, align_bytes=64)
-            nc.vector.quantize_mx(
-                out=codes[:].rearrange("p r g b -> p (r g b)").bitcast(FP8X4),
-                scales=scales[:].rearrange("p r g b -> p (r g b)"),
-                in_=grouped_of[i][:].rearrange("p r g b t -> p (r g b t)"),
-            )
+            grouped_of[i] = grouped
             codes_of[i] = codes
             scales_of[i] = scales
+
+        def regroup(copy, i, r):
+            copy(
+                out=grouped_of[i][:].bitcast(F32)[:, r, :, :, :],
+                in_=banks[(i, r)][:].rearrange("p (g u) b -> p g b u", u=HALVES),
+            )
+
+        def quantise(i, rows):
+            nc.vector.quantize_mx(
+                out=codes_of[i][:, rows, :, :].rearrange("p r g b -> p (r g b)").bitcast(FP8X4),
+                scales=scales_of[i][:, rows, :, :].rearrange("p r g b -> p (r g b)"),
+                in_=grouped_of[i][:, rows, :, :, :].rearrange("p r g b t -> p (r g b t)"),
+            )
+
+        def column_pieces(i, r):
+            return HALVED if (i, r) == (GROUPS - 1, GROUP - 1) else WHOLE
 
         def matmuls(i):
             for r in range(GROUP):
                 acc = psum_acc.tile([P, FEAT], F32, tag="acc")
-                for g in range(PASSES):
-                    nc.tensor.matmul_mx(
-                        out=acc[:],
-                        lhsT=codes_of[i][:, r, g, :].bitcast(FP8X4),
-                        lhsT_scale=scales_of[i][:, r, g, :],
-                        rhs=w_codes[:, g, :].bitcast(FP8X4),
-                        rhs_scale=w_scales[:, g, :],
-                        start=(g == 0),
-                        stop=(g == PASSES - 1),
-                    )
+                for cols in column_pieces(i, r):
+                    for g in range(PASSES):
+                        nc.tensor.matmul_mx(
+                            out=acc[:, cols],
+                            lhsT=codes_of[i][:, r, g, :].bitcast(FP8X4),
+                            lhsT_scale=scales_of[i][:, r, g, :],
+                            rhs=w_codes[:, g, cols].bitcast(FP8X4),
+                            rhs_scale=w_scales[:, g, cols],
+                            start=(g == 0),
+                            stop=(g == PASSES - 1),
+                        )
                 acc_of[(i, r)] = acc
 
         def add_bias(i):
             z = results.tile([P, GROUP, FEAT], F32)
             for r in range(GROUP):
-                nc.vector.tensor_tensor(out=z[:, r, :], in0=acc_of[(i, r)][:], in1=bias[:], op=ADD)
+                for cols in column_pieces(i, r):
+                    nc.vector.tensor_tensor(out=z[:, r, cols], in0=acc_of[(i, r)][:, cols], in1=bias[:, cols], op=ADD)
             z_of[i] = z
 
         def gate(i):
             for r in range(GROUP):
-                nc.scalar.activation(out=z_of[i][:, r, :], in_=z_of[i][:, r, :], func=SIGMOID)
+                for cols in column_pieces(i, r):
+                    nc.scalar.activation(out=z_of[i][:, r, cols], in_=z_of[i][:, r, cols], func=SIGMOID)
 
         def multiply_and_store(i):
             z = z_of[i]
             engines = (nc.vector if i == GROUPS - 1 else nc.gpsimd, nc.vector)
             for r in range(GROUP):
-                engines[r].tensor_tensor(out=z[:, r, :], in0=z[:, r, :], in1=m_groups[i][:, r, :], op=MULT)
-                nc.sync.dma_start(out=out_rows[:, i * GROUP + r, :], in_=z[:, r, :])
+                for cols in column_pieces(i, r):
+                    engines[r].tensor_tensor(
+                        out=z[:, r, cols], in0=z[:, r, cols], in1=m_groups[i][:, r, cols], op=MULT
+                    )
+                    nc.sync.dma_start(out=out_rows[:, i * GROUP + r, cols], in_=z[:, r, cols])
 
         transposes(0)
-        regroup(0)
-        quantise(0)
+        stage_tiles(0)
+        quantise_w(0)
+        quantise_w(1)
+        quantise_w(2)
+        regroup(nc.vector.tensor_copy, 0, 0)
+        regroup(nc.scalar.copy, 0, 1)
+        quantise_w(3)
+        for r in range(GROUP):
+            quantise(0, slice(r, r + 1))
+
+        bias_sum = psum_acc.tile([P, FEAT], F32, tag="acc")
+        nc.tensor.matmul(out=bias_sum[:], lhsT=ones[:], rhs=bias_row[:], start=True, stop=True)
+        bias = consts.tile([P, FEAT], F32)
+        nc.scalar.copy(out=bias[:], in_=bias_sum[:])
+
         for i in range(GROUPS + 1):
             if i + 1 < GROUPS:
                 transposes(i + 1)
             if i < GROUPS:
                 matmuls(i)
             if i + 1 < GROUPS:
-                regroup(i + 1)
+                stage_tiles(i + 1)
+                for r in range(GROUP):
+                    regroup(nc.scalar.copy, i + 1, r)
             if i >= 1:
                 gate(i - 1)
             if i + 1 < GROUPS:
-                quantise(i + 1)
+                quantise(i + 1, slice(0, GROUP))
             if i < GROUPS:
                 add_bias(i)
             if i >= 1:

@@ -41,7 +41,7 @@ def tile_dynamicmemorycell_pa_t_kernel(tc, input_tensor, previous_memory, fg_w, 
         consts = ctx.enter_context(tc.tile_pool(name="consts", bufs=1))
         inputs = ctx.enter_context(tc.tile_pool(name="inputs", bufs=GROUPS))
         stage = ctx.enter_context(tc.tile_pool(name="stage", bufs=3))
-        results = ctx.enter_context(tc.tile_pool(name="results", bufs=GROUPS // 2))
+        results = ctx.enter_context(tc.tile_pool(name="results", bufs=GROUPS))
         psum_t = ctx.enter_context(tc.psum_pool(name="psum_t", bufs=2 * GROUP))
         psum_acc = ctx.enter_context(tc.psum_pool(name="psum_acc", bufs=2 * GROUP))
         ctx.enter_context(tc.manual_schedule())
@@ -189,7 +189,7 @@ def tile_dynamicmemorycell_pa_t_kernel(tc, input_tensor, previous_memory, fg_w, 
         bias_sum = psum_acc.tile([P, FEAT], F32, tag="acc")
         nc.tensor.matmul(out=bias_sum[:], lhsT=ones[:], rhs=bias_row[:], start=True, stop=True)
         bias = consts.tile([P, FEAT], F32)
-        nc.scalar.copy(out=bias[:], in_=bias_sum[:])
+        nc.vector.tensor_copy(out=bias[:], in_=bias_sum[:])
 
         for i in range(GROUPS + 1):
             if i + 1 < GROUPS:

@@ -24,8 +24,8 @@ ROWS_PER_PARTITION = BATCH // P
 GROUP = 2
 GROUPS = ROWS_PER_PARTITION // GROUP
 N_TILES = FEAT // P
-WHOLE = (slice(0, FEAT),)
-HALVED = (slice(0, FEAT // 2), slice(FEAT // 2, FEAT))
+HALF = FEAT // 2
+LAST = GROUPS - 1
 
 FLOPS = 2 * BATCH * (PASSES * FEAT) * FEAT
 
@@ -41,7 +41,7 @@ def tile_dynamicmemorycell_pa_t_kernel(tc, input_tensor, previous_memory, fg_w, 
         consts = ctx.enter_context(tc.tile_pool(name="consts", bufs=1))
         inputs = ctx.enter_context(tc.tile_pool(name="inputs", bufs=GROUPS))
         stage = ctx.enter_context(tc.tile_pool(name="stage", bufs=3))
-        results = ctx.enter_context(tc.tile_pool(name="results", bufs=GROUPS))
+        results = ctx.enter_context(tc.tile_pool(name="results", bufs=GROUPS // 2))
         psum_t = ctx.enter_context(tc.psum_pool(name="psum_t", bufs=2 * GROUP))
         psum_acc = ctx.enter_context(tc.psum_pool(name="psum_acc", bufs=2 * GROUP))
         ctx.enter_context(tc.manual_schedule())
@@ -114,16 +114,18 @@ def tile_dynamicmemorycell_pa_t_kernel(tc, input_tensor, previous_memory, fg_w, 
                 banks[(i, r)] = xt
 
         def stage_tiles(i):
-            grouped = stage.tile([P, GROUP, PASSES, P, PACK], BF16, align_bytes=64)
-            codes = stage.tile([P, GROUP, PASSES, P], U32, align_bytes=64)
-            scales = stage.tile([P, GROUP, PASSES, P], U8, align_bytes=64)
+            order = [PASSES, GROUP] if i == LAST else [GROUP, PASSES]
+            grouped = stage.tile([P] + order + [P, PACK], BF16, align_bytes=64)
+            codes = stage.tile([P] + order + [P], U32, align_bytes=64)
+            scales = stage.tile([P] + order + [P], U8, align_bytes=64)
             grouped_of[i] = grouped
             codes_of[i] = codes
             scales_of[i] = scales
 
         def regroup(copy, i, r):
+            words = grouped_of[i][:].bitcast(F32)
             copy(
-                out=grouped_of[i][:].bitcast(F32)[:, r, :, :, :],
+                out=words[:, :, r, :, :] if i == LAST else words[:, r, :, :, :],
                 in_=banks[(i, r)][:].rearrange("p (g u) b -> p g b u", u=HALVES),
             )
 
@@ -134,46 +136,95 @@ def tile_dynamicmemorycell_pa_t_kernel(tc, input_tensor, previous_memory, fg_w, 
                 in_=grouped_of[i][:, rows, :, :, :].rearrange("p r g b t -> p (r g b t)"),
             )
 
-        def column_pieces(i, r):
-            return HALVED if (i, r) == (GROUPS - 1, GROUP - 1) else WHOLE
-
         def matmuls(i):
             for r in range(GROUP):
                 acc = psum_acc.tile([P, FEAT], F32, tag="acc")
-                for cols in column_pieces(i, r):
-                    for g in range(PASSES):
-                        nc.tensor.matmul_mx(
-                            out=acc[:, cols],
-                            lhsT=codes_of[i][:, r, g, :].bitcast(FP8X4),
-                            lhsT_scale=scales_of[i][:, r, g, :],
-                            rhs=w_codes[:, g, cols].bitcast(FP8X4),
-                            rhs_scale=w_scales[:, g, cols],
-                            start=(g == 0),
-                            stop=(g == PASSES - 1),
-                        )
+                for g in range(PASSES):
+                    nc.tensor.matmul_mx(
+                        out=acc[:],
+                        lhsT=codes_of[i][:, r, g, :].bitcast(FP8X4),
+                        lhsT_scale=scales_of[i][:, r, g, :],
+                        rhs=w_codes[:, g, :].bitcast(FP8X4),
+                        rhs_scale=w_scales[:, g, :],
+                        start=(g == 0),
+                        stop=(g == PASSES - 1),
+                    )
                 acc_of[(i, r)] = acc
 
         def add_bias(i):
             z = results.tile([P, GROUP, FEAT], F32)
             for r in range(GROUP):
-                for cols in column_pieces(i, r):
-                    nc.vector.tensor_tensor(out=z[:, r, cols], in0=acc_of[(i, r)][:, cols], in1=bias[:, cols], op=ADD)
+                nc.vector.tensor_tensor(out=z[:, r, :], in0=acc_of[(i, r)][:], in1=bias[:], op=ADD)
             z_of[i] = z
 
-        def gate(i):
-            for r in range(GROUP):
-                for cols in column_pieces(i, r):
-                    nc.scalar.activation(out=z_of[i][:, r, cols], in_=z_of[i][:, r, cols], func=SIGMOID)
+        def gate(i, r):
+            nc.scalar.activation(out=z_of[i][:, r, :], in_=z_of[i][:, r, :], func=SIGMOID)
 
         def multiply_and_store(i):
             z = z_of[i]
-            engines = (nc.vector if i == GROUPS - 1 else nc.gpsimd, nc.vector)
+            engines = (nc.gpsimd, nc.vector)
             for r in range(GROUP):
-                for cols in column_pieces(i, r):
-                    engines[r].tensor_tensor(
-                        out=z[:, r, cols], in0=z[:, r, cols], in1=m_groups[i][:, r, cols], op=MULT
+                engines[r].tensor_tensor(out=z[:, r, :], in0=z[:, r, :], in1=m_groups[i][:, r, :], op=MULT)
+                nc.sync.dma_start(out=out_rows[:, i * GROUP + r, :], in_=z[:, r, :])
+
+        def multiply_and_store_piece(i, r, cols):
+            z = z_of[i]
+            nc.vector.tensor_tensor(out=z[:, r, cols], in0=z[:, r, cols], in1=m_groups[i][:, r, cols], op=MULT)
+            nc.sync.dma_start(out=out_rows[:, i * GROUP + r, cols], in_=z[:, r, cols])
+
+        bias_column = consts.tile([P, N_TILES], F32)
+        gate_t = consts.tile([P, N_TILES, GROUP, P], F32)
+        z_last = consts.tile([P, 2, GROUP, HALF], F32)
+        sums_t = {}
+        gate_banks = {}
+
+        def make_bias_column():
+            bt = psum_t.tile([P, N_TILES, P], F32, tag="xt")
+            for j in range(N_TILES):
+                nc.tensor.transpose(bt[:, j, :], bias[:, j * P : (j + 1) * P], ident[:])
+            nc.scalar.copy(out=bias_column[:], in_=bt[:, :, 0])
+
+        def matmuls_last():
+            for j in range(N_TILES):
+                if j % 2 == 0:
+                    acc = psum_acc.tile([P, FEAT], F32, tag="acc")
+                half = slice(j % 2 * HALF, (j % 2 + 1) * HALF)
+                features = slice(j * P, (j + 1) * P)
+                for g in range(PASSES):
+                    nc.tensor.matmul_mx(
+                        out=acc[:, half],
+                        lhsT=w_codes[:, g, features].bitcast(FP8X4),
+                        lhsT_scale=w_scales[:, g, features],
+                        rhs=codes_of[LAST][:, g, :, :].rearrange("p r b -> p (r b)").bitcast(FP8X4),
+                        rhs_scale=scales_of[LAST][:, g, :, :].rearrange("p r b -> p (r b)"),
+                        start=(g == 0),
+                        stop=(g == PASSES - 1),
                     )
-                    nc.sync.dma_start(out=out_rows[:, i * GROUP + r, cols], in_=z[:, r, cols])
+                sums_t[j] = acc[:, half]
+
+        def gate_last(j):
+            nc.scalar.activation(
+                out=gate_t[:, j, :, :].rearrange("p r b -> p (r b)"),
+                in_=sums_t[j],
+                func=SIGMOID,
+                bias=bias_column[:, j : j + 1],
+            )
+
+        def transpose_gate_back(j):
+            if j % 2 == 0:
+                bank = psum_t.tile([P, GROUP, HALF], F32, tag="xt")
+                gate_banks[j // 2] = bank
+            for r in range(GROUP):
+                nc.tensor.transpose(
+                    gate_banks[j // 2][:, r, j % 2 * P : (j % 2 + 1) * P], gate_t[:, j, r, :], ident[:]
+                )
+
+        def multiply_and_store_last(half):
+            cols = slice(half * HALF, (half + 1) * HALF)
+            nc.vector.tensor_tensor(
+                out=z_last[:, half, :, :], in0=gate_banks[half][:], in1=m_groups[LAST][:, :, cols], op=MULT
+            )
+            nc.sync.dma_start(out=out_rows[:, LAST * GROUP : (LAST + 1) * GROUP, cols], in_=z_last[:, half, :, :])
 
         transposes(0)
         stage_tiles(0)
@@ -191,20 +242,29 @@ def tile_dynamicmemorycell_pa_t_kernel(tc, input_tensor, previous_memory, fg_w, 
         bias = consts.tile([P, FEAT], F32)
         nc.vector.tensor_copy(out=bias[:], in_=bias_sum[:])
 
-        for i in range(GROUPS + 1):
-            if i + 1 < GROUPS:
-                transposes(i + 1)
-            if i < GROUPS:
-                matmuls(i)
-            if i + 1 < GROUPS:
-                stage_tiles(i + 1)
-                for r in range(GROUP):
-                    regroup(nc.scalar.copy, i + 1, r)
+        for i in range(LAST):
+            transposes(i + 1)
+            matmuls(i)
+            stage_tiles(i + 1)
+            for r in range(GROUP):
+                regroup(nc.scalar.copy, i + 1, r)
             if i >= 1:
-                gate(i - 1)
-            if i + 1 < GROUPS:
-                quantise(i + 1, slice(0, GROUP))
-            if i < GROUPS:
-                add_bias(i)
+                for r in range(GROUP):
+                    gate(i - 1, r)
+            quantise(i + 1, slice(0, GROUP))
+            add_bias(i)
             if i >= 1:
                 multiply_and_store(i - 1)
+
+        make_bias_column()
+        matmuls_last()
+        gate(LAST - 1, 0)
+        for j in range(N_TILES):
+            gate_last(j)
+            transpose_gate_back(j)
+        gate(LAST - 1, 1)
+        multiply_and_store_piece(LAST - 1, 0, slice(0, FEAT))
+        multiply_and_store_last(0)
+        multiply_and_store_last(1)
+        multiply_and_store_piece(LAST - 1, 1, slice(0, HALF))
+        multiply_and_store_piece(LAST - 1, 1, slice(HALF, FEAT))

@@ -136,8 +136,8 @@ def tile_dynamicmemorycell_pa_t_kernel(tc, input_tensor, previous_memory, fg_w, 
                 in_=grouped_of[i][:, rows, :, :, :].rearrange("p r g b t -> p (r g b t)"),
             )
 
-        def matmuls(i):
-            for r in range(GROUP):
+        def matmuls(i, row_tiles):
+            for r in row_tiles:
                 acc = psum_acc.tile([P, FEAT], F32, tag="acc")
                 for g in range(PASSES):
                     nc.tensor.matmul_mx(
@@ -243,8 +243,15 @@ def tile_dynamicmemorycell_pa_t_kernel(tc, input_tensor, previous_memory, fg_w, 
         nc.vector.tensor_copy(out=bias[:], in_=bias_sum[:])
 
         for i in range(LAST):
-            transposes(i + 1)
-            matmuls(i)
+            if i == 0:
+                transposes(1)
+                matmuls(0, range(1))
+                transposes(2)
+                matmuls(0, range(1, GROUP))
+            else:
+                if i >= 2:
+                    transposes(i + 1)
+                matmuls(i, range(GROUP))
             stage_tiles(i + 1)
             for r in range(GROUP):
                 regroup(nc.scalar.copy, i + 1, r)
@@ -260,11 +267,11 @@ def tile_dynamicmemorycell_pa_t_kernel(tc, input_tensor, previous_memory, fg_w, 
         matmuls_last()
         gate(LAST - 1, 0)
         for j in range(N_TILES):
+            if j == N_TILES // 2:
+                gate(LAST - 1, 1)
             gate_last(j)
             transpose_gate_back(j)
-        gate(LAST - 1, 1)
         multiply_and_store_piece(LAST - 1, 0, slice(0, FEAT))
         multiply_and_store_last(0)
+        multiply_and_store_piece(LAST - 1, 1, slice(0, FEAT))
         multiply_and_store_last(1)
-        multiply_and_store_piece(LAST - 1, 1, slice(0, HALF))
-        multiply_and_store_piece(LAST - 1, 1, slice(HALF, FEAT))

from contextlib import ExitStack

import concourse.mybir as mybir
from concourse.masks import make_identity

F32 = mybir.dt.float32
BF16 = mybir.dt.bfloat16
U32 = mybir.dt.uint32
U8 = mybir.dt.uint8
FP8X4 = mybir.dt.float8_e4m3fn_x4
ADD = mybir.AluOpType.add
MULT = mybir.AluOpType.mult
SIGMOID = mybir.ActivationFunctionType.Sigmoid

P = 128
BATCH = 4096
FEAT = 512
PASSES = 2
PACK = 4
HALVES = 2
BLOCKS = PASSES * HALVES
PASS_WORDS = FEAT // 2
ROWS_PER_PARTITION = BATCH // P
GROUP = 2
GROUPS = ROWS_PER_PARTITION // GROUP
N_TILES = FEAT // P
HALF = FEAT // 2
LAST = GROUPS - 1

FLOPS = 2 * BATCH * (PASSES * FEAT) * FEAT


def tile_dynamicmemorycell_pa_t_kernel(tc, input_tensor, previous_memory, fg_w, fg_b, out):
    nc = tc.nc

    m_rows = previous_memory.rearrange("(p r) k -> p r k", r=ROWS_PER_PARTITION)
    x_rows = input_tensor.rearrange("(p r) k -> p r k", r=ROWS_PER_PARTITION)
    out_rows = out.rearrange("(p r) n -> p r n", r=ROWS_PER_PARTITION)

    with ExitStack() as ctx:
        consts = ctx.enter_context(tc.tile_pool(name="consts", bufs=1))
        inputs = ctx.enter_context(tc.tile_pool(name="inputs", bufs=GROUPS))
        stage = ctx.enter_context(tc.tile_pool(name="stage", bufs=3))
        results = ctx.enter_context(tc.tile_pool(name="results", bufs=GROUPS // 2))
        psum_t = ctx.enter_context(tc.psum_pool(name="psum_t", bufs=2 * GROUP))
        psum_acc = ctx.enter_context(tc.psum_pool(name="psum_acc", bufs=2 * GROUP))
        ctx.enter_context(tc.manual_schedule())

        w_sb = consts.tile([P, N_TILES, PASSES * FEAT], BF16)
        for j in range(N_TILES):
            nc.sync.dma_start(out=w_sb[:, j, :], in_=fg_w[j * P : (j + 1) * P, :])
        bias_row = consts.tile([P, FEAT], BF16)
        nc.vector.memset(bias_row[:], 0.0)
        m_groups = []
        x_groups = []
        for i in range(GROUPS):
            rows = slice(i * GROUP, (i + 1) * GROUP)
            m_sb = inputs.tile([P, GROUP, FEAT], BF16)
            nc.sync.dma_start(out=m_sb[:], in_=m_rows[:, rows, :])
            x_sb = inputs.tile([P, GROUP, FEAT], BF16)
            nc.sync.dma_start(out=x_sb[:], in_=x_rows[:, rows, :])
            m_groups.append(m_sb)
            x_groups.append(x_sb)
            if i == 0:
                nc.sync.dma_start(out=bias_row[0:1, :], in_=fg_b.rearrange("(o n) -> o n", o=1))

        ident = consts.tile([P, P], F32)
        make_identity(nc, ident[:])
        ones = consts.tile([P, P], BF16)
        nc.vector.memset(ones[:], 1.0)
        warm = consts.tile([P, 1], F32)
        nc.vector.memset(warm[:], 0.0)
        nc.scalar.activation(out=warm[:], in_=warm[:], func=SIGMOID)

        w_words = w_sb[:].bitcast(F32)
        w_grouped = consts.tile([P, N_TILES, PASSES, P, PACK], BF16, align_bytes=64)
        w_grouped_words = w_grouped[:].bitcast(F32)
        for j in range(N_TILES):
            wt = psum_t.tile([P, BLOCKS, P], F32, tag="xt")
            for g in range(PASSES):
                for u in range(HALVES):
                    words = w_words[:, j, g * PASS_WORDS + u : (g + 1) * PASS_WORDS : HALVES]
                    nc.tensor.transpose(wt[:, g * HALVES + u, :], words, ident[:])
            nc.scalar.copy(
                out=w_grouped_words[:, j, :, :, :],
                in_=wt[:].rearrange("p (g u) n -> p g n u", u=HALVES),
            )
        w_codes = consts.tile([P, PASSES, FEAT], U32, align_bytes=64)
        w_scales = consts.tile([P, PASSES, FEAT], U8, align_bytes=64)

        def quantise_w(j):
            cols = slice(j * P, (j + 1) * P)
            for g in range(PASSES):
                nc.vector.quantize_mx(
                    out=w_codes[:, g, cols].bitcast(FP8X4),
                    scales=w_scales[:, g, cols],
                    in_=w_grouped[:, j, g, :, :].rearrange("p n t -> p (n t)"),
                )

        banks = {}
        grouped_of = {}
        codes_of = {}
        scales_of = {}
        acc_of = {}
        z_of = {}

        def transposes(i):
            for r in range(GROUP):
                xt = psum_t.tile([P, BLOCKS, P], F32, tag="xt")
                for g, src in enumerate((m_groups[i], x_groups[i])):
                    words = src[:].bitcast(F32)
                    for u in range(HALVES):
                        nc.tensor.transpose(xt[:, g * HALVES + u, :], words[:, r, u:PASS_WORDS:HALVES], ident[:])
                banks[(i, r)] = xt

        def stage_tiles(i):
            order = [PASSES, GROUP] if i == LAST else [GROUP, PASSES]
            grouped = stage.tile([P] + order + [P, PACK], BF16, align_bytes=64)
            codes = stage.tile([P] + order + [P], U32, align_bytes=64)
            scales = stage.tile([P] + order + [P], U8, align_bytes=64)
            grouped_of[i] = grouped
            codes_of[i] = codes
            scales_of[i] = scales

        def regroup(copy, i, r):
            words = grouped_of[i][:].bitcast(F32)
            copy(
                out=words[:, :, r, :, :] if i == LAST else words[:, r, :, :, :],
                in_=banks[(i, r)][:].rearrange("p (g u) b -> p g b u", u=HALVES),
            )

        def quantise(i, rows):
            nc.vector.quantize_mx(
                out=codes_of[i][:, rows, :, :].rearrange("p r g b -> p (r g b)").bitcast(FP8X4),
                scales=scales_of[i][:, rows, :, :].rearrange("p r g b -> p (r g b)"),
                in_=grouped_of[i][:, rows, :, :, :].rearrange("p r g b t -> p (r g b t)"),
            )

        def matmuls(i, row_tiles):
            for r in row_tiles:
                acc = psum_acc.tile([P, FEAT], F32, tag="acc")
                for g in range(PASSES):
                    nc.tensor.matmul_mx(
                        out=acc[:],
                        lhsT=codes_of[i][:, r, g, :].bitcast(FP8X4),
                        lhsT_scale=scales_of[i][:, r, g, :],
                        rhs=w_codes[:, g, :].bitcast(FP8X4),
                        rhs_scale=w_scales[:, g, :],
                        start=(g == 0),
                        stop=(g == PASSES - 1),
                    )
                acc_of[(i, r)] = acc

        def add_bias(i):
            z = results.tile([P, GROUP, FEAT], F32)
            for r in range(GROUP):
                nc.vector.tensor_tensor(out=z[:, r, :], in0=acc_of[(i, r)][:], in1=bias[:], op=ADD)
            z_of[i] = z

        def gate(i, r):
            nc.scalar.activation(out=z_of[i][:, r, :], in_=z_of[i][:, r, :], func=SIGMOID)

        def multiply_and_store(i):
            z = z_of[i]
            engines = (nc.gpsimd, nc.vector)
            for r in range(GROUP):
                engines[r].tensor_tensor(out=z[:, r, :], in0=z[:, r, :], in1=m_groups[i][:, r, :], op=MULT)
                nc.sync.dma_start(out=out_rows[:, i * GROUP + r, :], in_=z[:, r, :])

        def multiply_and_store_piece(i, r, cols):
            z = z_of[i]
            nc.vector.tensor_tensor(out=z[:, r, cols], in0=z[:, r, cols], in1=m_groups[i][:, r, cols], op=MULT)
            nc.sync.dma_start(out=out_rows[:, i * GROUP + r, cols], in_=z[:, r, cols])

        bias_column = consts.tile([P, N_TILES], F32)
        gate_t = consts.tile([P, N_TILES, GROUP, P], F32)
        z_last = consts.tile([P, 2, GROUP, HALF], F32)
        sums_t = {}
        gate_banks = {}

        def make_bias_column():
            bt = psum_t.tile([P, N_TILES, P], F32, tag="xt")
            for j in range(N_TILES):
                nc.tensor.transpose(bt[:, j, :], bias[:, j * P : (j + 1) * P], ident[:])
            nc.scalar.copy(out=bias_column[:], in_=bt[:, :, 0])

        def matmuls_last():
            for j in range(N_TILES):
                if j % 2 == 0:
                    acc = psum_acc.tile([P, FEAT], F32, tag="acc")
                half = slice(j % 2 * HALF, (j % 2 + 1) * HALF)
                features = slice(j * P, (j + 1) * P)
                for g in range(PASSES):
                    nc.tensor.matmul_mx(
                        out=acc[:, half],
                        lhsT=w_codes[:, g, features].bitcast(FP8X4),
                        lhsT_scale=w_scales[:, g, features],
                        rhs=codes_of[LAST][:, g, :, :].rearrange("p r b -> p (r b)").bitcast(FP8X4),
                        rhs_scale=scales_of[LAST][:, g, :, :].rearrange("p r b -> p (r b)"),
                        start=(g == 0),
                        stop=(g == PASSES - 1),
                    )
                sums_t[j] = acc[:, half]

        def gate_last(j):
            nc.scalar.activation(
                out=gate_t[:, j, :, :].rearrange("p r b -> p (r b)"),
                in_=sums_t[j],
                func=SIGMOID,
                bias=bias_column[:, j : j + 1],
            )

        def transpose_gate_back(j):
            if j % 2 == 0:
                bank = psum_t.tile([P, GROUP, HALF], F32, tag="xt")
                gate_banks[j // 2] = bank
            for r in range(GROUP):
                nc.tensor.transpose(
                    gate_banks[j // 2][:, r, j % 2 * P : (j % 2 + 1) * P], gate_t[:, j, r, :], ident[:]
                )

        def multiply_and_store_last(half):
            cols = slice(half * HALF, (half + 1) * HALF)
            nc.vector.tensor_tensor(
                out=z_last[:, half, :, :], in0=gate_banks[half][:], in1=m_groups[LAST][:, :, cols], op=MULT
            )
            nc.sync.dma_start(out=out_rows[:, LAST * GROUP : (LAST + 1) * GROUP, cols], in_=z_last[:, half, :, :])

        transposes(0)
        stage_tiles(0)
        quantise_w(0)
        quantise_w(1)
        quantise_w(2)
        regroup(nc.vector.tensor_copy, 0, 0)
        regroup(nc.scalar.copy, 0, 1)
        quantise_w(3)
        for r in range(GROUP):
            quantise(0, slice(r, r + 1))

        bias_sum = psum_acc.tile([P, FEAT], F32, tag="acc")
        nc.tensor.matmul(out=bias_sum[:], lhsT=ones[:], rhs=bias_row[:], start=True, stop=True)
        bias = consts.tile([P, FEAT], F32)
        nc.vector.tensor_copy(out=bias[:], in_=bias_sum[:])

        for i in range(LAST):
            if i == 0:
                transposes(1)
                matmuls(0, range(1))
                transposes(2)
                matmuls(0, range(1, GROUP))
            else:
                if i >= 2:
                    transposes(i + 1)
                matmuls(i, range(GROUP))
            stage_tiles(i + 1)
            for r in range(GROUP):
                regroup(nc.scalar.copy, i + 1, r)
            if i >= 1:
                for r in range(GROUP):
                    gate(i - 1, r)
            quantise(i + 1, slice(0, GROUP))
            add_bias(i)
            if i >= 1:
                multiply_and_store(i - 1)

        make_bias_column()
        matmuls_last()
        gate(LAST - 1, 0)
        for j in range(N_TILES):
            if j == N_TILES // 2:
                gate(LAST - 1, 1)
            gate_last(j)
            transpose_gate_back(j)
        multiply_and_store_piece(LAST - 1, 0, slice(0, FEAT))
        multiply_and_store_last(0)
        multiply_and_store_piece(LAST - 1, 1, slice(0, FEAT))
        multiply_and_store_last(1)
